import numpy as np
import ml_dtypes


def mxq(x, axis, fmt="e4m3"):
    dtype, down = {"e4m3": (ml_dtypes.float8_e4m3fn, 7), "e5m2": (ml_dtypes.float8_e5m2, 14)}[fmt]
    v = np.moveaxis(np.asarray(x, np.float32).astype(ml_dtypes.bfloat16).astype(np.float64), axis, -1)
    blocks = v.reshape(v.shape[:-1] + (-1, 32))
    amax = np.abs(blocks).max(-1, keepdims=True)
    byte = np.maximum(np.where(amax > 0, np.frexp(amax)[1] - 1 + 127, 0) - down, 1)
    scale = np.exp2(byte - 127.0)
    codes = (blocks / scale).astype(np.float32).astype(dtype).astype(np.float64)
    return np.moveaxis((codes * scale).reshape(v.shape), -1, axis)


WIDE = False


def mx_kscale(k):
    if not WIDE:
        return np.ones(k)
    levels = np.array([20, -20, 10, -10, 0])
    a = np.random.permutation(np.resize(levels, k // 512 * 4)).reshape(k // 512, 4)
    idx = np.arange(k)
    return np.exp2(a[idx // 512, idx % 128 // 32])


BF16 = ml_dtypes.bfloat16


def bf(x):
    return np.asarray(x, np.float32).astype(BF16)


def f64(x):
    return np.asarray(x).astype(np.float64)


B, C, CK, CV, CO, H, W, P1, P2, P3, P4 = 2, 512, 256, 256, 1024, 48, 32, 1, 3, 6, 8
EPS = 1e-5
N = H * W
CF = C + C


def pre_relu(ctx_attn, feats, Ww, bw, Wo, bo, go, betao, mo, vo):
    ctx = f64(Ww) @ f64(ctx_attn).reshape(B, CV, N) + f64(bw)[None, :, None]
    fused = np.concatenate([ctx, f64(feats).reshape(B, C, N)], axis=1)
    y = f64(Wo) @ fused + f64(bo)[None, :, None]
    k = f64(go) / np.sqrt(f64(vo) + EPS)
    return ((y - f64(mo)[None, :, None]) * k[None, :, None] + f64(betao)[None, :, None]).reshape(B, CO, H, W)


def setup_inputs():
    u = mx_kscale(CO)
    ctx_attn = bf(np.random.standard_normal((B, CV, H, W)) * 0.4)
    feats = bf(np.random.standard_normal((B, C, H, W)))
    Ww = bf(np.random.standard_normal((C, CV)) * 2.5 / np.sqrt(CV))
    bw = bf(np.random.standard_normal(C) * 0.2)
    Wo0 = bf(np.random.standard_normal((CO, CF)) / np.sqrt(CF))
    bo = bf(np.random.standard_normal(CO) * 0.2)
    go = bf(1.0 + 0.1 * np.random.standard_normal(CO))
    betao = bf(np.random.standard_normal(CO) * 0.2)
    mo = bf(np.random.standard_normal(CO) * 0.2)
    vo = bf(np.random.uniform(0.5, 1.5, CO))
    g = bf(np.random.standard_normal((B, CO, H, W)) * np.exp2(np.random.randint(-12, 1, (B, 1, H, W))) * 8.0 * u[None, :, None, None])
    z = pre_relu(ctx_attn, feats, Ww, bw, Wo0, bo, go, betao, mo, vo)
    return {"ctx_attn": ctx_attn, "feats": feats, "Ww": Ww, "bw": bw,
            "Wo": bf(f64(Wo0) / u[:, None]), "bo": bo, "go": go, "betao": betao, "mo": mo, "vo": vo,
            "z": np.asarray(z, np.float32), "grad_out": g}


def reference(ctx_attn, feats, Ww, bw, Wo, bo, go, betao, mo, vo, z, grad_out):
    k = f64(go) / np.sqrt(f64(vo) + EPS)
    dy = f64(grad_out).reshape(B, CO, N) * (f64(z).reshape(B, CO, N) > 0.0) * k[None, :, None]
    dy2 = dy.transpose(1, 0, 2).reshape(CO, B * N)
    wf = f64(Wo)[:, C:]
    gx = mxq(wf, 0, "e4m3").T @ mxq(dy2, 0, "e5m2")
    return gx.reshape(C, B, N).transpose(1, 0, 2).reshape(B, C, H, W)

@@ -1,0 +1,133 @@
+from contextlib import ExitStack
+
+import concourse.mybir as mybir
+
+F32 = mybir.dt.float32
+BF16 = mybir.dt.bfloat16
+U32 = mybir.dt.uint32
+U8 = mybir.dt.uint8
+E4M3_X4 = mybir.dt.float8_e4m3fn_x4
+E5M2_X4 = mybir.dt.float8_e5m2_x4
+ALU = mybir.AluOpType
+ACT = mybir.ActivationFunctionType
+
+IMAGES = 2
+CHANNELS = 1024
+FEATS = 512
+POSITIONS = 48 * 32
+EPS = 1e-5
+
+P = 128
+PACK = 4
+K_PASS = P * PACK
+PASSES = CHANNELS // K_PASS
+N_TILE = 512
+CHUNKS = POSITIONS // N_TILE
+M_TILE = 128
+M_TILES = FEATS // M_TILE
+
+FLOPS = 2 * CHANNELS * FEATS * IMAGES * POSITIONS
+BYTES = IMAGES * CHANNELS * POSITIONS * (4 + 2) + CHANNELS * FEATS * 2 + 2 * CHANNELS * 2 + IMAGES * FEATS * POSITIONS * 4
+
+
+def tile_apnb_pb_t_v_kernel(tc, ctx_attn, feats, Ww, bw, Wo, bo, go, betao, mo, vo, z, grad_out, out):
+    nc = tc.nc
+
+    g_view = grad_out.rearrange("b (c p j) h w -> b c p j (h w)", c=PASSES, p=P, j=PACK)
+    z_view = z.rearrange("b (c p j) h w -> b c p j (h w)", c=PASSES, p=P, j=PACK)
+    w_view = Wo.rearrange("(c p j) f -> c p j f", c=PASSES, p=P, j=PACK)
+    go_view = go.rearrange("(c p j) -> p c j", c=PASSES, p=P, j=PACK)
+    vo_view = vo.rearrange("(c p j) -> p c j", c=PASSES, p=P, j=PACK)
+    out_view = out.rearrange("b (m p) h w -> b p m (h w)", m=M_TILES, p=P)
+
+    with ExitStack() as ctx:
+        keep = ctx.enter_context(tc.tile_pool(name="keep", bufs=1))
+        g_pool = ctx.enter_context(tc.tile_pool(name="g", bufs=IMAGES * PASSES))
+        wide_pool = ctx.enter_context(tc.tile_pool(name="wide", bufs=IMAGES * PASSES * CHUNKS))
+        work = ctx.enter_context(tc.tile_pool(name="work", bufs=3))
+        mx_pool = ctx.enter_context(tc.tile_pool(name="mx", bufs=IMAGES * PASSES * CHUNKS))
+        psum = ctx.enter_context(tc.psum_pool(name="psum", bufs=2 * M_TILES))
+
+        go_sb = keep.tile([P, PASSES, PACK], BF16)
+        vo_sb = keep.tile([P, PASSES, PACK], BF16)
+        nc.scalar.dma_start(out=vo_sb[:], in_=vo_view)
+        nc.scalar.dma_start(out=go_sb[:], in_=go_view)
+        var_eps = keep.tile([P, PASSES, PACK], F32)
+        nc.vector.tensor_scalar_add(out=var_eps[:], in0=vo_sb[:], scalar1=EPS)
+        std = keep.tile([P, PASSES, PACK], F32)
+        nc.scalar.activation(out=std[:], in_=var_eps[:], func=ACT.Sqrt)
+        inv_std = keep.tile([P, PASSES, PACK], F32)
+        nc.vector.reciprocal(out=inv_std[:], in_=std[:])
+        factor = keep.tile([P, PASSES, PACK], F32)
+        nc.vector.tensor_mul(out=factor[:], in0=go_sb[:], in1=inv_std[:])
+
+        w_raw = keep.tile([P, PASSES, PACK, FEATS], BF16)
+        for c in range(PASSES):
+            nc.sync.dma_start(out=w_raw[:, c], in_=w_view[c][:, :, FEATS : 2 * FEATS])
+        g_sb = {}
+        z_sb = {}
+        for b in range(IMAGES):
+            for c in range(PASSES):
+                g_sb[b, c] = g_pool.tile([P, PACK, POSITIONS], BF16, name="g_sb")
+                nc.sync.dma_start(out=g_sb[b, c][:], in_=g_view[b, c])
+                for n in range(CHUNKS):
+                    z_sb[b, c, n] = wide_pool.tile([P, PACK, N_TILE], F32, name="z_sb", tag="wide")
+                    nc.sync.dma_start(out=z_sb[b, c, n][:], in_=z_view[b, c][:, :, n * N_TILE : (n + 1) * N_TILE])
+
+        w_codes = keep.tile([P, PASSES, FEATS], U32, align_bytes=64)
+        w_scales = keep.tile([P, PASSES, FEATS], U8, align_bytes=64)
+        for c in range(PASSES):
+            w_grouped = work.tile([P, FEATS, PACK], BF16, tag="grouped", align_bytes=64)
+            nc.vector.tensor_copy(out=w_grouped[:], in_=w_raw[:, c].rearrange("p j f -> p f j"))
+            nc.vector.quantize_mx(
+                out=w_codes[:, c, :].bitcast(E4M3_X4),
+                scales=w_scales[:, c, :],
+                in_=w_grouped[:].rearrange("p f j -> p (f j)"),
+            )
+
+        for b in range(IMAGES):
+            dy_codes = {}
+            dy_scales = {}
+            for c in range(PASSES):
+                for n in range(CHUNKS):
+                    cols = slice(n * N_TILE, (n + 1) * N_TILE)
+                    scaled = work.tile([P, PACK, N_TILE], BF16)
+                    for j in range(PACK):
+                        nc.scalar.activation(
+                            out=scaled[:, j, :], in_=g_sb[b, c][:, j, cols], func=ACT.Copy, scale=factor[:, c, j : j + 1]
+                        )
+                    dy = work.tile([P, N_TILE, PACK], BF16, tag="grouped", align_bytes=64)
+                    nc.vector.scalar_tensor_tensor(
+                        out=dy[:],
+                        in0=z_sb[b, c, n][:].rearrange("p j w -> p w j"),
+                        scalar=0.0,
+                        in1=scaled[:].rearrange("p j w -> p w j"),
+                        op0=ALU.is_gt,
+                        op1=ALU.mult,
+                    )
+                    dy_codes[c, n] = mx_pool.tile([P, N_TILE], U32, name="dy_codes", align_bytes=64)
+                    dy_scales[c, n] = mx_pool.tile([P, N_TILE], U8, name="dy_scales", align_bytes=64)
+                    nc.vector.quantize_mx(
+                        out=dy_codes[c, n][:].bitcast(E5M2_X4),
+                        scales=dy_scales[c, n][:],
+                        in_=dy[:].rearrange("p w j -> p (w j)"),
+                    )
+
+            for n in range(CHUNKS):
+                accs = [psum.tile([P, N_TILE], F32, name="acc") for m in range(M_TILES)]
+                for c in range(PASSES):
+                    for m in range(M_TILES):
+                        m_cols = slice(m * M_TILE, (m + 1) * M_TILE)
+                        nc.tensor.matmul_mx(
+                            out=accs[m][:],
+                            lhsT=w_codes[:, c, m_cols].bitcast(E4M3_X4),
+                            lhsT_scale=w_scales[:, c, m_cols],
+                            rhs=dy_codes[c, n][:].bitcast(E5M2_X4),
+                            rhs_scale=dy_scales[c, n][:],
+                            start=(c == 0),
+                            stop=(c == PASSES - 1),
+                        )
+                product = wide_pool.tile([P, M_TILES, N_TILE], F32, tag="wide")
+                for m in range(M_TILES):
+                    nc.scalar.copy(out=product[:, m, :], in_=accs[m][:])
+                nc.sync.dma_start(out=out_view[b][:, :, n * N_TILE : (n + 1) * N_TILE], in_=product[:])

@@ -25,6 +25,7 @@ N_TILE = 512
 CHUNKS = POSITIONS // N_TILE
 M_TILE = 128
 M_TILES = FEATS // M_TILE
+AHEAD = 3
 
 FLOPS = 2 * CHANNELS * FEATS * IMAGES * POSITIONS
 BYTES = IMAGES * CHANNELS * POSITIONS * (4 + 2) + CHANNELS * FEATS * 2 + 2 * CHANNELS * 2 + IMAGES * FEATS * POSITIONS * 4
@@ -40,18 +41,35 @@ def tile_apnb_pb_t_v_kernel(tc, ctx_attn, feats, Ww, bw, Wo, bo, go, betao, mo, 
     vo_view = vo.rearrange("(c p j) -> p c j", c=PASSES, p=P, j=PACK)
     out_view = out.rearrange("b (m p) h w -> b p m (h w)", m=M_TILES, p=P)
 
+    pieces = [(b, c, n) for b in range(IMAGES) for c in range(PASSES) for n in range(CHUNKS)]
+
     with ExitStack() as ctx:
+        ctx.enter_context(tc.manual_schedule())
         keep = ctx.enter_context(tc.tile_pool(name="keep", bufs=1))
         g_pool = ctx.enter_context(tc.tile_pool(name="g", bufs=IMAGES * PASSES))
-        wide_pool = ctx.enter_context(tc.tile_pool(name="wide", bufs=IMAGES * PASSES * CHUNKS))
-        work = ctx.enter_context(tc.tile_pool(name="work", bufs=3))
-        mx_pool = ctx.enter_context(tc.tile_pool(name="mx", bufs=IMAGES * PASSES * CHUNKS))
+        wide_pool = ctx.enter_context(tc.tile_pool(name="wide", bufs=len(pieces)))
+        scaled_pool = ctx.enter_context(tc.tile_pool(name="scaled", bufs=AHEAD + 2))
+        grouped_pool = ctx.enter_context(tc.tile_pool(name="grouped", bufs=3))
+        mx_pool = ctx.enter_context(tc.tile_pool(name="mx", bufs=len(pieces)))
         psum = ctx.enter_context(tc.psum_pool(name="psum", bufs=2 * M_TILES))
 
         go_sb = keep.tile([P, PASSES, PACK], BF16)
         vo_sb = keep.tile([P, PASSES, PACK], BF16)
         nc.scalar.dma_start(out=vo_sb[:], in_=vo_view)
         nc.scalar.dma_start(out=go_sb[:], in_=go_view)
+        w_raw = {}
+        for c in range(PASSES):
+            w_raw[c] = keep.tile([P, PACK, FEATS], BF16, name="w_raw%d" % c)
+            nc.sync.dma_start(out=w_raw[c][:], in_=w_view[c][:, :, FEATS : 2 * FEATS])
+        g_sb = {}
+        z_sb = {}
+        for b, c, n in pieces:
+            if n == 0:
+                g_sb[b, c] = g_pool.tile([P, PACK, POSITIONS], BF16, name="g_sb")
+                nc.sync.dma_start(out=g_sb[b, c][:], in_=g_view[b, c])
+            z_sb[b, c, n] = wide_pool.tile([P, PACK, N_TILE], F32, name="z_sb", tag="wide")
+            nc.sync.dma_start(out=z_sb[b, c, n][:], in_=z_view[b, c][:, :, n * N_TILE : (n + 1) * N_TILE])
+
         var_eps = keep.tile([P, PASSES, PACK], F32)
         nc.vector.tensor_scalar_add(out=var_eps[:], in0=vo_sb[:], scalar1=EPS)
         std = keep.tile([P, PASSES, PACK], F32)
@@ -61,73 +79,86 @@ def tile_apnb_pb_t_v_kernel(tc, ctx_attn, feats, Ww, bw, Wo, bo, go, betao, mo, 
         factor = keep.tile([P, PASSES, PACK], F32)
         nc.vector.tensor_mul(out=factor[:], in0=go_sb[:], in1=inv_std[:])
 
-        w_raw = keep.tile([P, PASSES, PACK, FEATS], BF16)
-        for c in range(PASSES):
-            nc.sync.dma_start(out=w_raw[:, c], in_=w_view[c][:, :, FEATS : 2 * FEATS])
-        g_sb = {}
-        z_sb = {}
-        for b in range(IMAGES):
-            for c in range(PASSES):
-                g_sb[b, c] = g_pool.tile([P, PACK, POSITIONS], BF16, name="g_sb")
-                nc.sync.dma_start(out=g_sb[b, c][:], in_=g_view[b, c])
-                for n in range(CHUNKS):
-                    z_sb[b, c, n] = wide_pool.tile([P, PACK, N_TILE], F32, name="z_sb", tag="wide")
-                    nc.sync.dma_start(out=z_sb[b, c, n][:], in_=z_view[b, c][:, :, n * N_TILE : (n + 1) * N_TILE])
-
         w_codes = keep.tile([P, PASSES, FEATS], U32, align_bytes=64)
         w_scales = keep.tile([P, PASSES, FEATS], U8, align_bytes=64)
+        w_grouped = {}
         for c in range(PASSES):
-            w_grouped = work.tile([P, FEATS, PACK], BF16, tag="grouped", align_bytes=64)
-            nc.vector.tensor_copy(out=w_grouped[:], in_=w_raw[:, c].rearrange("p j f -> p f j"))
+            w_grouped[c] = grouped_pool.tile([P, FEATS, PACK], BF16, name="w_grouped", tag="grouped", align_bytes=64)
+            nc.vector.tensor_copy(out=w_grouped[c][:], in_=w_raw[c][:].rearrange("p j f -> p f j"))
+        for c in range(PASSES):
             nc.vector.quantize_mx(
                 out=w_codes[:, c, :].bitcast(E4M3_X4),
                 scales=w_scales[:, c, :],
-                in_=w_grouped[:].rearrange("p f j -> p (f j)"),
+                in_=w_grouped[c][:].rearrange("p f j -> p (f j)"),
             )
 
-        for b in range(IMAGES):
-            dy_codes = {}
-            dy_scales = {}
+        scaled = {}
+        dy = {}
+        dy_codes = {}
+        dy_scales = {}
+
+        def scale(piece):
+            b, c, n = piece
+            scaled[piece] = scaled_pool.tile([P, PACK, N_TILE], BF16, name="scaled")
+            for j in range(PACK):
+                nc.scalar.activation(
+                    out=scaled[piece][:, j, :],
+                    in_=g_sb[b, c][:, j, n * N_TILE : (n + 1) * N_TILE],
+                    func=ACT.Copy,
+                    scale=factor[:, c, j : j + 1],
+                )
+
+        def mask(piece):
+            dy[piece] = grouped_pool.tile([P, N_TILE, PACK], BF16, name="dy", tag="grouped", align_bytes=64)
+            nc.vector.scalar_tensor_tensor(
+                out=dy[piece][:],
+                in0=z_sb[piece][:].rearrange("p j w -> p w j"),
+                scalar=0.0,
+                in1=scaled[piece][:].rearrange("p j w -> p w j"),
+                op0=ALU.is_gt,
+                op1=ALU.mult,
+            )
+
+        def quantise(piece):
+            dy_codes[piece] = mx_pool.tile([P, N_TILE], U32, name="dy_codes", align_bytes=64)
+            dy_scales[piece] = mx_pool.tile([P, N_TILE], U8, name="dy_scales", align_bytes=64)
+            nc.vector.quantize_mx(
+                out=dy_codes[piece][:].bitcast(E5M2_X4),
+                scales=dy_scales[piece][:],
+                in_=dy[piece][:].rearrange("p w j -> p (w j)"),
+            )
+
+        def multiply(b, n):
+            accs = [psum.tile([P, N_TILE], F32, name="acc") for m in range(M_TILES)]
             for c in range(PASSES):
-                for n in range(CHUNKS):
-                    cols = slice(n * N_TILE, (n + 1) * N_TILE)
-                    scaled = work.tile([P, PACK, N_TILE], BF16)
-                    for j in range(PACK):
-                        nc.scalar.activation(
-                            out=scaled[:, j, :], in_=g_sb[b, c][:, j, cols], func=ACT.Copy, scale=factor[:, c, j : j + 1]
-                        )
-                    dy = work.tile([P, N_TILE, PACK], BF16, tag="grouped", align_bytes=64)
-                    nc.vector.scalar_tensor_tensor(
-                        out=dy[:],
-                        in0=z_sb[b, c, n][:].rearrange("p j w -> p w j"),
-                        scalar=0.0,
-                        in1=scaled[:].rearrange("p j w -> p w j"),
-                        op0=ALU.is_gt,
-                        op1=ALU.mult,
+                for m in range(M_TILES):
+                    m_cols = slice(m * M_TILE, (m + 1) * M_TILE)
+                    nc.tensor.matmul_mx(
+                        out=accs[m][:],
+                        lhsT=w_codes[:, c, m_cols].bitcast(E4M3_X4),
+                        lhsT_scale=w_scales[:, c, m_cols],
+                        rhs=dy_codes[b, c, n][:].bitcast(E5M2_X4),
+                        rhs_scale=dy_scales[b, c, n][:],
+                        start=(c == 0),
+                        stop=(c == PASSES - 1),
                     )
-                    dy_codes[c, n] = mx_pool.tile([P, N_TILE], U32, name="dy_codes", align_bytes=64)
-                    dy_scales[c, n] = mx_pool.tile([P, N_TILE], U8, name="dy_scales", align_bytes=64)
-                    nc.vector.quantize_mx(
-                        out=dy_codes[c, n][:].bitcast(E5M2_X4),
-                        scales=dy_scales[c, n][:],
-                        in_=dy[:].rearrange("p w j -> p (w j)"),
+            product = wide_pool.tile([P, M_TILES, N_TILE], F32, tag="wide")
+            for m in range(M_TILES):
+                nc.scalar.copy(out=product[:, m, :], in_=accs[m][:])
+                if m % 2 == 1:
+                    nc.sync.dma_start(
+                        out=out_view[b][:, m - 1 : m + 1, n * N_TILE : (n + 1) * N_TILE], in_=product[:, m - 1 : m + 1, :]
                     )
 
-            for n in range(CHUNKS):
-                accs = [psum.tile([P, N_TILE], F32, name="acc") for m in range(M_TILES)]
-                for c in range(PASSES):
-                    for m in range(M_TILES):
-                        m_cols = slice(m * M_TILE, (m + 1) * M_TILE)
-                        nc.tensor.matmul_mx(
-                            out=accs[m][:],
-                            lhsT=w_codes[:, c, m_cols].bitcast(E4M3_X4),
-                            lhsT_scale=w_scales[:, c, m_cols],
-                            rhs=dy_codes[c, n][:].bitcast(E5M2_X4),
-                            rhs_scale=dy_scales[c, n][:],
-                            start=(c == 0),
-                            stop=(c == PASSES - 1),
-                        )
-                product = wide_pool.tile([P, M_TILES, N_TILE], F32, tag="wide")
-                for m in range(M_TILES):
-                    nc.scalar.copy(out=product[:, m, :], in_=accs[m][:])
-                nc.sync.dma_start(out=out_view[b][:, :, n * N_TILE : (n + 1) * N_TILE], in_=product[:])
+        for piece in pieces[:AHEAD]:
+            scale(piece)
+        for i in range(len(pieces) + 1):
+            if i + AHEAD < len(pieces):
+                scale(pieces[i + AHEAD])
+            if i < len(pieces):
+                mask(pieces[i])
+            if i > 0:
+                quantise(pieces[i - 1])
+                b, c, n = pieces[i - 1]
+                if c == PASSES - 1:
+                    multiply(b, n)

@@ -26,6 +26,7 @@ CHUNKS = POSITIONS // N_TILE
 M_TILE = 128
 M_TILES = FEATS // M_TILE
 AHEAD = 3
+OPEN_CHUNKS = 2
 
 FLOPS = 2 * CHANNELS * FEATS * IMAGES * POSITIONS
 BYTES = IMAGES * CHANNELS * POSITIONS * (4 + 2) + CHANNELS * FEATS * 2 + 2 * CHANNELS * 2 + IMAGES * FEATS * POSITIONS * 4
@@ -51,7 +52,7 @@ def tile_apnb_pb_t_v_kernel(tc, ctx_attn, feats, Ww, bw, Wo, bo, go, betao, mo, 
         scaled_pool = ctx.enter_context(tc.tile_pool(name="scaled", bufs=AHEAD + 2))
         grouped_pool = ctx.enter_context(tc.tile_pool(name="grouped", bufs=3))
         mx_pool = ctx.enter_context(tc.tile_pool(name="mx", bufs=len(pieces)))
-        psum = ctx.enter_context(tc.psum_pool(name="psum", bufs=2 * M_TILES))
+        psum = ctx.enter_context(tc.psum_pool(name="psum", bufs=OPEN_CHUNKS * M_TILES))
 
         go_sb = keep.tile([P, PASSES, PACK], BF16)
         vo_sb = keep.tile([P, PASSES, PACK], BF16)
@@ -128,27 +129,45 @@ def tile_apnb_pb_t_v_kernel(tc, ctx_attn, feats, Ww, bw, Wo, bo, go, betao, mo, 
                 in_=dy[piece][:].rearrange("p w j -> p (w j)"),
             )
 
-        def multiply(b, n):
-            accs = [psum.tile([P, N_TILE], F32, name="acc") for m in range(M_TILES)]
-            for c in range(PASSES):
-                for m in range(M_TILES):
-                    m_cols = slice(m * M_TILE, (m + 1) * M_TILE)
-                    nc.tensor.matmul_mx(
-                        out=accs[m][:],
-                        lhsT=w_codes[:, c, m_cols].bitcast(E4M3_X4),
-                        lhsT_scale=w_scales[:, c, m_cols],
-                        rhs=dy_codes[b, c, n][:].bitcast(E5M2_X4),
-                        rhs_scale=dy_scales[b, c, n][:],
-                        start=(c == 0),
-                        stop=(c == PASSES - 1),
-                    )
+        accs = {}
+
+        def passes(b, c, n):
+            if c == 0:
+                accs[b, n] = [psum.tile([P, N_TILE], F32, name="acc") for m in range(M_TILES)]
+            for m in range(M_TILES):
+                m_cols = slice(m * M_TILE, (m + 1) * M_TILE)
+                nc.tensor.matmul_mx(
+                    out=accs[b, n][m][:],
+                    lhsT=w_codes[:, c, m_cols].bitcast(E4M3_X4),
+                    lhsT_scale=w_scales[:, c, m_cols],
+                    rhs=dy_codes[b, c, n][:].bitcast(E5M2_X4),
+                    rhs_scale=dy_scales[b, c, n][:],
+                    start=(c == 0),
+                    stop=(c == PASSES - 1),
+                )
+
+        def empty(b, n, shared):
             product = wide_pool.tile([P, M_TILES, N_TILE], F32, tag="wide")
             for m in range(M_TILES):
-                nc.scalar.copy(out=product[:, m, :], in_=accs[m][:])
+                if shared and m >= M_TILES // 2:
+                    nc.vector.tensor_copy(out=product[:, m, :], in_=accs[b, n][m][:])
+                else:
+                    nc.scalar.copy(out=product[:, m, :], in_=accs[b, n][m][:])
                 if m % 2 == 1:
                     nc.sync.dma_start(
                         out=out_view[b][:, m - 1 : m + 1, n * N_TILE : (n + 1) * N_TILE], in_=product[:, m - 1 : m + 1, :]
                     )
+
+        chunks = [(b, n) for b in range(IMAGES) for n in range(CHUNKS)]
+        emptied = []
+        waiting = []
+
+        def open_chunks():
+            for b, n in list(waiting):
+                k = chunks.index((b, n))
+                if k < OPEN_CHUNKS or chunks[k - OPEN_CHUNKS] in emptied:
+                    passes(b, 0, n)
+                    waiting.remove((b, n))
 
         for piece in pieces[:AHEAD]:
             scale(piece)
@@ -160,5 +179,19 @@ def tile_apnb_pb_t_v_kernel(tc, ctx_attn, feats, Ww, bw, Wo, bo, go, betao, mo, 
             if i > 0:
                 quantise(pieces[i - 1])
                 b, c, n = pieces[i - 1]
-                if c == PASSES - 1:
-                    multiply(b, n)
+                if c == 0:
+                    waiting.append((b, n))
+                    open_chunks()
+                if i == len(pieces) - 1:
+                    held = (b, n)
+                elif c == PASSES - 1:
+                    if i == len(pieces):
+                        passes(held[0], c, held[1])
+                        passes(b, c, n)
+                        empty(held[0], held[1], True)
+                        empty(b, n, True)
+                    else:
+                        passes(b, c, n)
+                        empty(b, n, False)
+                        emptied.append((b, n))
+                        open_chunks()

@@ -48,7 +48,7 @@ def tile_apnb_pb_t_v_kernel(tc, ctx_attn, feats, Ww, bw, Wo, bo, go, betao, mo, 
         ctx.enter_context(tc.manual_schedule())
         keep = ctx.enter_context(tc.tile_pool(name="keep", bufs=1))
         g_pool = ctx.enter_context(tc.tile_pool(name="g", bufs=IMAGES * PASSES))
-        wide_pool = ctx.enter_context(tc.tile_pool(name="wide", bufs=len(pieces)))
+        wide_pool = ctx.enter_context(tc.tile_pool(name="wide", bufs=IMAGES * PASSES))
         scaled_pool = ctx.enter_context(tc.tile_pool(name="scaled", bufs=AHEAD + 2))
         grouped_pool = ctx.enter_context(tc.tile_pool(name="grouped", bufs=3))
         mx_pool = ctx.enter_context(tc.tile_pool(name="mx", bufs=len(pieces)))
@@ -68,8 +68,9 @@ def tile_apnb_pb_t_v_kernel(tc, ctx_attn, feats, Ww, bw, Wo, bo, go, betao, mo, 
             if n == 0:
                 g_sb[b, c] = g_pool.tile([P, PACK, POSITIONS], BF16, name="g_sb")
                 nc.sync.dma_start(out=g_sb[b, c][:], in_=g_view[b, c])
-            z_sb[b, c, n] = wide_pool.tile([P, PACK, N_TILE], F32, name="z_sb", tag="wide")
-            nc.sync.dma_start(out=z_sb[b, c, n][:], in_=z_view[b, c][:, :, n * N_TILE : (n + 1) * N_TILE])
+                z_sb[b, c] = wide_pool.tile([P, PACK, POSITIONS], F32, name="z_sb", tag="wide")
+            n_cols = slice(n * N_TILE, (n + 1) * N_TILE)
+            nc.sync.dma_start(out=z_sb[b, c][:, :, n_cols], in_=z_view[b, c][:, :, n_cols])
 
         var_eps = keep.tile([P, PASSES, PACK], F32)
         nc.vector.tensor_scalar_add(out=var_eps[:], in0=vo_sb[:], scalar1=EPS)
@@ -110,10 +111,11 @@ def tile_apnb_pb_t_v_kernel(tc, ctx_attn, feats, Ww, bw, Wo, bo, go, betao, mo, 
                 )
 
         def mask(piece):
+            b, c, n = piece
             dy[piece] = grouped_pool.tile([P, N_TILE, PACK], BF16, name="dy", tag="grouped", align_bytes=64)
             nc.vector.scalar_tensor_tensor(
                 out=dy[piece][:],
-                in0=z_sb[piece][:].rearrange("p j w -> p w j"),
+                in0=z_sb[b, c][:, :, n * N_TILE : (n + 1) * N_TILE].rearrange("p j w -> p w j"),
                 scalar=0.0,
                 in1=scaled[piece][:].rearrange("p j w -> p w j"),
                 op0=ALU.is_gt,
@@ -130,6 +132,7 @@ def tile_apnb_pb_t_v_kernel(tc, ctx_attn, feats, Ww, bw, Wo, bo, go, betao, mo, 
             )
 
         accs = {}
+        products = {}
 
         def passes(b, c, n):
             if c == 0:
@@ -147,16 +150,17 @@ def tile_apnb_pb_t_v_kernel(tc, ctx_attn, feats, Ww, bw, Wo, bo, go, betao, mo, 
                 )
 
         def empty(b, n, shared):
-            product = wide_pool.tile([P, M_TILES, N_TILE], F32, tag="wide")
+            if n == 0:
+                products[b] = wide_pool.tile([P, M_TILES, POSITIONS], F32, name="product", tag="wide")
+            product = products[b]
+            n_cols = slice(n * N_TILE, (n + 1) * N_TILE)
             for m in range(M_TILES):
                 if shared and m >= M_TILES // 2:
-                    nc.vector.tensor_copy(out=product[:, m, :], in_=accs[b, n][m][:])
+                    nc.vector.tensor_copy(out=product[:, m, n_cols], in_=accs[b, n][m][:])
                 else:
-                    nc.scalar.copy(out=product[:, m, :], in_=accs[b, n][m][:])
+                    nc.scalar.copy(out=product[:, m, n_cols], in_=accs[b, n][m][:])
                 if m % 2 == 1:
-                    nc.sync.dma_start(
-                        out=out_view[b][:, m - 1 : m + 1, n * N_TILE : (n + 1) * N_TILE], in_=product[:, m - 1 : m + 1, :]
-                    )
+                    nc.sync.dma_start(out=out_view[b][:, m - 1 : m + 1, n_cols], in_=product[:, m - 1 : m + 1, n_cols])
 
         chunks = [(b, n) for b in range(IMAGES) for n in range(CHUNKS)]
         emptied = []

@@ -25,7 +25,7 @@ N_TILE = 512
 CHUNKS = POSITIONS // N_TILE
 M_TILE = 128
 M_TILES = FEATS // M_TILE
-AHEAD = 3
+SCALED = 6
 OPEN_CHUNKS = 2
 
 FLOPS = 2 * CHANNELS * FEATS * IMAGES * POSITIONS
@@ -49,7 +49,7 @@ def tile_apnb_pb_t_v_kernel(tc, ctx_attn, feats, Ww, bw, Wo, bo, go, betao, mo, 
         keep = ctx.enter_context(tc.tile_pool(name="keep", bufs=1))
         g_pool = ctx.enter_context(tc.tile_pool(name="g", bufs=IMAGES * PASSES))
         wide_pool = ctx.enter_context(tc.tile_pool(name="wide", bufs=IMAGES * PASSES))
-        scaled_pool = ctx.enter_context(tc.tile_pool(name="scaled", bufs=AHEAD + 2))
+        scaled_pool = ctx.enter_context(tc.tile_pool(name="scaled", bufs=SCALED))
         grouped_pool = ctx.enter_context(tc.tile_pool(name="grouped", bufs=3))
         mx_pool = ctx.enter_context(tc.tile_pool(name="mx", bufs=len(pieces)))
         psum = ctx.enter_context(tc.psum_pool(name="psum", bufs=OPEN_CHUNKS * M_TILES))
@@ -149,53 +149,75 @@ def tile_apnb_pb_t_v_kernel(tc, ctx_attn, feats, Ww, bw, Wo, bo, go, betao, mo, 
                     stop=(c == PASSES - 1),
                 )
 
-        def empty(b, n, shared):
-            if n == 0:
-                products[b] = wide_pool.tile([P, M_TILES, POSITIONS], F32, name="product", tag="wide")
+        def empty(b, n, halves, engine):
+            if (b, n) not in started:
+                started.append((b, n))
+                if n == 0:
+                    products[b] = wide_pool.tile([P, M_TILES, POSITIONS], F32, name="product", tag="wide")
             product = products[b]
             n_cols = slice(n * N_TILE, (n + 1) * N_TILE)
-            for m in range(M_TILES):
-                if shared and m >= M_TILES // 2:
-                    nc.vector.tensor_copy(out=product[:, m, n_cols], in_=accs[b, n][m][:])
-                else:
-                    nc.scalar.copy(out=product[:, m, n_cols], in_=accs[b, n][m][:])
-                if m % 2 == 1:
-                    nc.sync.dma_start(out=out_view[b][:, m - 1 : m + 1, n_cols], in_=product[:, m - 1 : m + 1, n_cols])
-
-        chunks = [(b, n) for b in range(IMAGES) for n in range(CHUNKS)]
-        emptied = []
-        waiting = []
-
-        def open_chunks():
-            for b, n in list(waiting):
-                k = chunks.index((b, n))
-                if k < OPEN_CHUNKS or chunks[k - OPEN_CHUNKS] in emptied:
-                    passes(b, 0, n)
-                    waiting.remove((b, n))
-
-        for piece in pieces[:AHEAD]:
-            scale(piece)
-        for i in range(len(pieces) + 1):
-            if i + AHEAD < len(pieces):
-                scale(pieces[i + AHEAD])
-            if i < len(pieces):
-                mask(pieces[i])
-            if i > 0:
-                quantise(pieces[i - 1])
-                b, c, n = pieces[i - 1]
-                if c == 0:
-                    waiting.append((b, n))
-                    open_chunks()
-                if i == len(pieces) - 1:
-                    held = (b, n)
-                elif c == PASSES - 1:
-                    if i == len(pieces):
-                        passes(held[0], c, held[1])
-                        passes(b, c, n)
-                        empty(held[0], held[1], True)
-                        empty(b, n, True)
+            for half in halves:
+                for m in (2 * half, 2 * half + 1):
+                    if engine == "vector":
+                        nc.vector.tensor_copy(out=product[:, m, n_cols], in_=accs[b, n][m][:])
                     else:
-                        passes(b, c, n)
-                        empty(b, n, False)
-                        emptied.append((b, n))
-                        open_chunks()
+                        nc.scalar.copy(out=product[:, m, n_cols], in_=accs[b, n][m][:])
+                nc.sync.dma_start(
+                    out=out_view[b][:, 2 * half : 2 * half + 2, n_cols], in_=product[:, 2 * half : 2 * half + 2, n_cols]
+                )
+
+        def scale_group(b, c):
+            for n in range(CHUNKS):
+                scale((b, c, n))
+
+        started = []
+
+        scale_group(0, 0)
+        scale_group(0, 1)
+        mask((0, 0, 0))
+        mask((0, 0, 1))
+        quantise((0, 0, 0))
+        passes(0, 0, 0)
+        mask((0, 0, 2))
+        quantise((0, 0, 1))
+        passes(0, 0, 1)
+        mask((0, 1, 0))
+        quantise((0, 0, 2))
+        mask((0, 1, 1))
+        quantise((0, 1, 0))
+        passes(0, 1, 0)
+        empty(0, 0, (0,), "scalar")
+        scale_group(1, 0)
+        empty(0, 0, (1,), "scalar")
+        mask((0, 1, 2))
+        quantise((0, 1, 1))
+        passes(0, 1, 1)
+        passes(0, 0, 2)
+        empty(0, 1, (0, 1), "scalar")
+        mask((1, 0, 0))
+        quantise((0, 1, 2))
+        passes(0, 1, 2)
+        empty(0, 2, (0,), "scalar")
+        scale_group(1, 1)
+        empty(0, 2, (1,), "scalar")
+        mask((1, 0, 1))
+        quantise((1, 0, 0))
+        passes(1, 0, 0)
+        mask((1, 0, 2))
+        quantise((1, 0, 1))
+        passes(1, 0, 1)
+        mask((1, 1, 0))
+        quantise((1, 0, 2))
+        mask((1, 1, 1))
+        quantise((1, 1, 0))
+        passes(1, 1, 0)
+        empty(1, 0, (0, 1), "scalar")
+        quantise((1, 1, 1))
+        passes(1, 1, 1)
+        passes(1, 0, 2)
+        empty(1, 1, (0, 1), "scalar")
+        mask((1, 1, 2))
+        quantise((1, 1, 2))
+        passes(1, 1, 2)
+        empty(1, 2, (0,), "scalar")
+        empty(1, 2, (1,), "vector")

@@ -149,28 +149,26 @@ def tile_apnb_pb_t_v_kernel(tc, ctx_attn, feats, Ww, bw, Wo, bo, go, betao, mo, 
                     stop=(c == PASSES - 1),
                 )
 
-        def empty(b, n, halves, engine):
-            if (b, n) not in started:
-                started.append((b, n))
-                if n == 0:
-                    products[b] = wide_pool.tile([P, M_TILES, POSITIONS], F32, name="product", tag="wide")
-            product = products[b]
+        def empty(b, n, banks, engine):
+            if n == 0 and b not in products:
+                products[b] = wide_pool.tile([P, M_TILES, POSITIONS], F32, name="product", tag="wide")
             n_cols = slice(n * N_TILE, (n + 1) * N_TILE)
-            for half in halves:
-                for m in (2 * half, 2 * half + 1):
-                    if engine == "vector":
-                        nc.vector.tensor_copy(out=product[:, m, n_cols], in_=accs[b, n][m][:])
-                    else:
-                        nc.scalar.copy(out=product[:, m, n_cols], in_=accs[b, n][m][:])
-                nc.sync.dma_start(
-                    out=out_view[b][:, 2 * half : 2 * half + 2, n_cols], in_=product[:, 2 * half : 2 * half + 2, n_cols]
-                )
+            for m in banks:
+                if engine == "vector":
+                    nc.vector.tensor_copy(out=products[b][:, m, n_cols], in_=accs[b, n][m][:])
+                else:
+                    nc.scalar.copy(out=products[b][:, m, n_cols], in_=accs[b, n][m][:])
+
+        def store(queue, b, banks, first_chunk, last_chunk):
+            cols = slice(first_chunk * N_TILE, (last_chunk + 1) * N_TILE)
+            rows = slice(banks[0], banks[-1] + 1)
+            queue.dma_start(out=out_view[b][:, rows, cols], in_=products[b][:, rows, cols])
 
         def scale_group(b, c):
             for n in range(CHUNKS):
                 scale((b, c, n))
 
-        started = []
+        ALL = (0, 1, 2, 3)
 
         scale_group(0, 0)
         scale_group(0, 1)
@@ -186,38 +184,51 @@ def tile_apnb_pb_t_v_kernel(tc, ctx_attn, feats, Ww, bw, Wo, bo, go, betao, mo, 
         mask((0, 1, 1))
         quantise((0, 1, 0))
         passes(0, 1, 0)
-        empty(0, 0, (0,), "scalar")
+        empty(0, 0, (0, 1), "scalar")
         scale_group(1, 0)
-        empty(0, 0, (1,), "scalar")
+        empty(0, 0, (2, 3), "scalar")
         mask((0, 1, 2))
         quantise((0, 1, 1))
         passes(0, 1, 1)
         passes(0, 0, 2)
-        empty(0, 1, (0, 1), "scalar")
+        empty(0, 1, ALL, "scalar")
+        store(nc.sync, 0, ALL, 0, 1)
         mask((1, 0, 0))
         quantise((0, 1, 2))
         passes(0, 1, 2)
-        empty(0, 2, (0,), "scalar")
+        empty(0, 2, (0, 1), "scalar")
         scale_group(1, 1)
-        empty(0, 2, (1,), "scalar")
+        empty(0, 2, (2, 3), "scalar")
+        store(nc.sync, 0, ALL, 2, 2)
         mask((1, 0, 1))
         quantise((1, 0, 0))
         passes(1, 0, 0)
         mask((1, 0, 2))
         quantise((1, 0, 1))
-        passes(1, 0, 1)
         mask((1, 1, 0))
         quantise((1, 0, 2))
-        mask((1, 1, 1))
         quantise((1, 1, 0))
         passes(1, 1, 0)
+        passes(1, 0, 1)
         empty(1, 0, (0, 1), "scalar")
+        store(nc.sync, 1, (0, 1), 0, 0)
+        empty(1, 0, (2, 3), "scalar")
+        store(nc.sync, 1, (2, 3), 0, 0)
+        mask((1, 1, 1))
         quantise((1, 1, 1))
         passes(1, 1, 1)
         passes(1, 0, 2)
         empty(1, 1, (0, 1), "scalar")
+        store(nc.sync, 1, (0, 1), 1, 1)
+        empty(1, 1, (2, 3), "scalar")
+        store(nc.sync, 1, (2, 3), 1, 1)
         mask((1, 1, 2))
         quantise((1, 1, 2))
         passes(1, 1, 2)
-        empty(1, 2, (0,), "scalar")
-        empty(1, 2, (1,), "vector")
+        for m in ALL:
+            if m % 2 == 0:
+                empty(1, 2, (m,), "scalar")
+                store(nc.sync, 1, (m,), 2, 2)
+            else:
+                empty(1, 2, (m,), "vector")
+                store(nc.sync, 1, (m,), 2, 2)

@@ -26,6 +26,7 @@ CHUNKS = POSITIONS // N_TILE
 M_TILE = 128
 M_TILES = FEATS // M_TILE
 SCALED = 6
+JOINED = (1, 0)
 OPEN_CHUNKS = 2
 
 FLOPS = 2 * CHANNELS * FEATS * IMAGES * POSITIONS
@@ -70,6 +71,11 @@ def tile_apnb_pb_t_v_kernel(tc, ctx_attn, feats, Ww, bw, Wo, bo, go, betao, mo, 
                 nc.sync.dma_start(out=g_sb[b, c][:], in_=g_view[b, c])
                 z_sb[b, c] = wide_pool.tile([P, PACK, POSITIONS], F32, name="z_sb", tag="wide")
             n_cols = slice(n * N_TILE, (n + 1) * N_TILE)
+            if (b, c) == JOINED:
+                if n == 2:
+                    continue
+                if n == 1:
+                    n_cols = slice(N_TILE, POSITIONS)
             nc.sync.dma_start(out=z_sb[b, c][:, :, n_cols], in_=z_view[b, c][:, :, n_cols])
 
         var_eps = keep.tile([P, PASSES, PACK], F32)
@@ -192,14 +198,16 @@ def tile_apnb_pb_t_v_kernel(tc, ctx_attn, feats, Ww, bw, Wo, bo, go, betao, mo, 
         passes(0, 1, 1)
         passes(0, 0, 2)
         empty(0, 1, ALL, "scalar")
-        store(nc.sync, 0, ALL, 0, 1)
         mask((1, 0, 0))
         quantise((0, 1, 2))
         passes(0, 1, 2)
         empty(0, 2, (0, 1), "scalar")
-        scale_group(1, 1)
+        store(nc.sync, 0, (0, 1), 0, CHUNKS - 1)
+        scale((1, 1, 0))
+        scale((1, 1, 1))
         empty(0, 2, (2, 3), "scalar")
-        store(nc.sync, 0, ALL, 2, 2)
+        store(nc.sync, 0, (2, 3), 0, CHUNKS - 1)
+        scale((1, 1, 2))
         mask((1, 0, 1))
         quantise((1, 0, 0))
         passes(1, 0, 0)

from contextlib import ExitStack

import concourse.mybir as mybir

F32 = mybir.dt.float32
BF16 = mybir.dt.bfloat16
U32 = mybir.dt.uint32
U8 = mybir.dt.uint8
E4M3_X4 = mybir.dt.float8_e4m3fn_x4
E5M2_X4 = mybir.dt.float8_e5m2_x4
ALU = mybir.AluOpType
ACT = mybir.ActivationFunctionType

IMAGES = 2
CHANNELS = 1024
FEATS = 512
POSITIONS = 48 * 32
EPS = 1e-5

P = 128
PACK = 4
K_PASS = P * PACK
PASSES = CHANNELS // K_PASS
N_TILE = 512
CHUNKS = POSITIONS // N_TILE
M_TILE = 128
M_TILES = FEATS // M_TILE
SCALED = 6
JOINED = (1, 0)
OPEN_CHUNKS = 2

FLOPS = 2 * CHANNELS * FEATS * IMAGES * POSITIONS
BYTES = IMAGES * CHANNELS * POSITIONS * (4 + 2) + CHANNELS * FEATS * 2 + 2 * CHANNELS * 2 + IMAGES * FEATS * POSITIONS * 4


def tile_apnb_pb_t_v_kernel(tc, ctx_attn, feats, Ww, bw, Wo, bo, go, betao, mo, vo, z, grad_out, out):
    nc = tc.nc

    g_view = grad_out.rearrange("b (c p j) h w -> b c p j (h w)", c=PASSES, p=P, j=PACK)
    z_view = z.rearrange("b (c p j) h w -> b c p j (h w)", c=PASSES, p=P, j=PACK)
    w_view = Wo.rearrange("(c p j) f -> c p j f", c=PASSES, p=P, j=PACK)
    go_view = go.rearrange("(c p j) -> p c j", c=PASSES, p=P, j=PACK)
    vo_view = vo.rearrange("(c p j) -> p c j", c=PASSES, p=P, j=PACK)
    out_view = out.rearrange("b (m p) h w -> b p m (h w)", m=M_TILES, p=P)

    pieces = [(b, c, n) for b in range(IMAGES) for c in range(PASSES) for n in range(CHUNKS)]

    with ExitStack() as ctx:
        ctx.enter_context(tc.manual_schedule())
        keep = ctx.enter_context(tc.tile_pool(name="keep", bufs=1))
        g_pool = ctx.enter_context(tc.tile_pool(name="g", bufs=IMAGES * PASSES))
        wide_pool = ctx.enter_context(tc.tile_pool(name="wide", bufs=IMAGES * PASSES))
        scaled_pool = ctx.enter_context(tc.tile_pool(name="scaled", bufs=SCALED))
        grouped_pool = ctx.enter_context(tc.tile_pool(name="grouped", bufs=3))
        mx_pool = ctx.enter_context(tc.tile_pool(name="mx", bufs=len(pieces)))
        psum = ctx.enter_context(tc.psum_pool(name="psum", bufs=OPEN_CHUNKS * M_TILES))

        go_sb = keep.tile([P, PASSES, PACK], BF16)
        vo_sb = keep.tile([P, PASSES, PACK], BF16)
        nc.scalar.dma_start(out=vo_sb[:], in_=vo_view)
        nc.scalar.dma_start(out=go_sb[:], in_=go_view)
        w_raw = {}
        for c in range(PASSES):
            w_raw[c] = keep.tile([P, PACK, FEATS], BF16, name="w_raw%d" % c)
            nc.sync.dma_start(out=w_raw[c][:], in_=w_view[c][:, :, FEATS : 2 * FEATS])
        g_sb = {}
        z_sb = {}
        for b, c, n in pieces:
            if n == 0:
                g_sb[b, c] = g_pool.tile([P, PACK, POSITIONS], BF16, name="g_sb")
                nc.sync.dma_start(out=g_sb[b, c][:], in_=g_view[b, c])
                z_sb[b, c] = wide_pool.tile([P, PACK, POSITIONS], F32, name="z_sb", tag="wide")
            n_cols = slice(n * N_TILE, (n + 1) * N_TILE)
            if (b, c) == JOINED:
                if n == 2:
                    continue
                if n == 1:
                    n_cols = slice(N_TILE, POSITIONS)
            nc.sync.dma_start(out=z_sb[b, c][:, :, n_cols], in_=z_view[b, c][:, :, n_cols])

        var_eps = keep.tile([P, PASSES, PACK], F32)
        nc.vector.tensor_scalar_add(out=var_eps[:], in0=vo_sb[:], scalar1=EPS)
        std = keep.tile([P, PASSES, PACK], F32)
        nc.scalar.activation(out=std[:], in_=var_eps[:], func=ACT.Sqrt)
        inv_std = keep.tile([P, PASSES, PACK], F32)
        nc.vector.reciprocal(out=inv_std[:], in_=std[:])
        factor = keep.tile([P, PASSES, PACK], F32)
        nc.vector.tensor_mul(out=factor[:], in0=go_sb[:], in1=inv_std[:])

        w_codes = keep.tile([P, PASSES, FEATS], U32, align_bytes=64)
        w_scales = keep.tile([P, PASSES, FEATS], U8, align_bytes=64)
        w_grouped = {}
        for c in range(PASSES):
            w_grouped[c] = grouped_pool.tile([P, FEATS, PACK], BF16, name="w_grouped", tag="grouped", align_bytes=64)
            nc.vector.tensor_copy(out=w_grouped[c][:], in_=w_raw[c][:].rearrange("p j f -> p f j"))
        for c in range(PASSES):
            nc.vector.quantize_mx(
                out=w_codes[:, c, :].bitcast(E4M3_X4),
                scales=w_scales[:, c, :],
                in_=w_grouped[c][:].rearrange("p f j -> p (f j)"),
            )

        scaled = {}
        dy = {}
        dy_codes = {}
        dy_scales = {}

        def scale(piece):
            b, c, n = piece
            scaled[piece] = scaled_pool.tile([P, PACK, N_TILE], BF16, name="scaled")
            for j in range(PACK):
                nc.scalar.activation(
                    out=scaled[piece][:, j, :],
                    in_=g_sb[b, c][:, j, n * N_TILE : (n + 1) * N_TILE],
                    func=ACT.Copy,
                    scale=factor[:, c, j : j + 1],
                )

        def mask(piece):
            b, c, n = piece
            dy[piece] = grouped_pool.tile([P, N_TILE, PACK], BF16, name="dy", tag="grouped", align_bytes=64)
            nc.vector.scalar_tensor_tensor(
                out=dy[piece][:],
                in0=z_sb[b, c][:, :, n * N_TILE : (n + 1) * N_TILE].rearrange("p j w -> p w j"),
                scalar=0.0,
                in1=scaled[piece][:].rearrange("p j w -> p w j"),
                op0=ALU.is_gt,
                op1=ALU.mult,
            )

        def quantise(piece):
            dy_codes[piece] = mx_pool.tile([P, N_TILE], U32, name="dy_codes", align_bytes=64)
            dy_scales[piece] = mx_pool.tile([P, N_TILE], U8, name="dy_scales", align_bytes=64)
            nc.vector.quantize_mx(
                out=dy_codes[piece][:].bitcast(E5M2_X4),
                scales=dy_scales[piece][:],
                in_=dy[piece][:].rearrange("p w j -> p (w j)"),
            )

        accs = {}
        products = {}

        def passes(b, c, n):
            if c == 0:
                accs[b, n] = [psum.tile([P, N_TILE], F32, name="acc") for m in range(M_TILES)]
            for m in range(M_TILES):
                m_cols = slice(m * M_TILE, (m + 1) * M_TILE)
                nc.tensor.matmul_mx(
                    out=accs[b, n][m][:],
                    lhsT=w_codes[:, c, m_cols].bitcast(E4M3_X4),
                    lhsT_scale=w_scales[:, c, m_cols],
                    rhs=dy_codes[b, c, n][:].bitcast(E5M2_X4),
                    rhs_scale=dy_scales[b, c, n][:],
                    start=(c == 0),
                    stop=(c == PASSES - 1),
                )

        def empty(b, n, banks, engine):
            if n == 0 and b not in products:
                products[b] = wide_pool.tile([P, M_TILES, POSITIONS], F32, name="product", tag="wide")
            n_cols = slice(n * N_TILE, (n + 1) * N_TILE)
            for m in banks:
                if engine == "vector":
                    nc.vector.tensor_copy(out=products[b][:, m, n_cols], in_=accs[b, n][m][:])
                else:
                    nc.scalar.copy(out=products[b][:, m, n_cols], in_=accs[b, n][m][:])

        def store(queue, b, banks, first_chunk, last_chunk):
            cols = slice(first_chunk * N_TILE, (last_chunk + 1) * N_TILE)
            rows = slice(banks[0], banks[-1] + 1)
            queue.dma_start(out=out_view[b][:, rows, cols], in_=products[b][:, rows, cols])

        def scale_group(b, c):
            for n in range(CHUNKS):
                scale((b, c, n))

        ALL = (0, 1, 2, 3)

        scale_group(0, 0)
        scale_group(0, 1)
        mask((0, 0, 0))
        mask((0, 0, 1))
        quantise((0, 0, 0))
        passes(0, 0, 0)
        mask((0, 0, 2))
        quantise((0, 0, 1))
        passes(0, 0, 1)
        mask((0, 1, 0))
        quantise((0, 0, 2))
        mask((0, 1, 1))
        quantise((0, 1, 0))
        passes(0, 1, 0)
        empty(0, 0, (0, 1), "scalar")
        scale_group(1, 0)
        empty(0, 0, (2, 3), "scalar")
        mask((0, 1, 2))
        quantise((0, 1, 1))
        passes(0, 1, 1)
        passes(0, 0, 2)
        empty(0, 1, ALL, "scalar")
        mask((1, 0, 0))
        quantise((0, 1, 2))
        passes(0, 1, 2)
        empty(0, 2, (0, 1), "scalar")
        store(nc.sync, 0, (0, 1), 0, CHUNKS - 1)
        scale((1, 1, 0))
        scale((1, 1, 1))
        empty(0, 2, (2, 3), "scalar")
        store(nc.sync, 0, (2, 3), 0, CHUNKS - 1)
        scale((1, 1, 2))
        mask((1, 0, 1))
        quantise((1, 0, 0))
        passes(1, 0, 0)
        mask((1, 0, 2))
        quantise((1, 0, 1))
        mask((1, 1, 0))
        quantise((1, 0, 2))
        quantise((1, 1, 0))
        passes(1, 1, 0)
        passes(1, 0, 1)
        empty(1, 0, (0, 1), "scalar")
        store(nc.sync, 1, (0, 1), 0, 0)
        empty(1, 0, (2, 3), "scalar")
        store(nc.sync, 1, (2, 3), 0, 0)
        mask((1, 1, 1))
        quantise((1, 1, 1))
        passes(1, 1, 1)
        passes(1, 0, 2)
        empty(1, 1, (0, 1), "scalar")
        store(nc.sync, 1, (0, 1), 1, 1)
        empty(1, 1, (2, 3), "scalar")
        store(nc.sync, 1, (2, 3), 1, 1)
        mask((1, 1, 2))
        quantise((1, 1, 2))
        passes(1, 1, 2)
        for m in ALL:
            if m % 2 == 0:
                empty(1, 2, (m,), "scalar")
                store(nc.sync, 1, (m,), 2, 2)
            else:
                empty(1, 2, (m,), "vector")
                store(nc.sync, 1, (m,), 2, 2)
